import numpy as np
import ml_dtypes


def mxq(x, axis, fmt="e4m3"):
    dtype, down = {"e4m3": (ml_dtypes.float8_e4m3fn, 7), "e5m2": (ml_dtypes.float8_e5m2, 14)}[fmt]
    v = np.moveaxis(np.asarray(x, np.float32).astype(ml_dtypes.bfloat16).astype(np.float64), axis, -1)
    blocks = v.reshape(v.shape[:-1] + (-1, 32))
    amax = np.abs(blocks).max(-1, keepdims=True)
    byte = np.maximum(np.where(amax > 0, np.frexp(amax)[1] - 1 + 127, 0) - down, 1)
    scale = np.exp2(byte - 127.0)
    codes = (blocks / scale).astype(np.float32).astype(dtype).astype(np.float64)
    return np.moveaxis((codes * scale).reshape(v.shape), -1, axis)


WIDE = False


def mx_kscale(k):
    if not WIDE:
        return np.ones(k)
    levels = np.array([10, -10, 5, -5, 0])
    a = np.random.permutation(np.resize(levels, k // 512 * 4)).reshape(k // 512, 4)
    idx = np.arange(k)
    return np.exp2(a[idx // 512, idx % 128 // 32])


BF16 = ml_dtypes.bfloat16


def bf(x):
    return np.asarray(x, np.float32).astype(BF16)


def f64(x):
    return np.asarray(x).astype(np.float64)


B, SQ, SK, D, DK, L = 2, 1024, 1024, 1024, 64, 10000
SCALE = np.sqrt(2.0 * DK)


def setup_inputs():
    s = mx_kscale(D)
    a = np.sqrt(1.4 * SCALE / np.sqrt(D))
    return {"q": bf(np.random.standard_normal((B, SQ, D)) * a * s),
            "k": bf(np.random.standard_normal((B, SK, D)) * a / s),
            "v": bf(np.random.standard_normal((B, SK, D)) * 2.0),
            "pos_bias": bf(np.random.standard_normal((SQ, SK)) * SCALE)}


def reference(q, k, v, pos_bias):
    scores = mxq(f64(q), 2, "e4m3") @ mxq(f64(k), 2, "e4m3").transpose(0, 2, 1)
    scores = scores + f64(pos_bias)[None, :, :]
    scores = scores / SCALE
    e = np.exp(scores - scores.max(-1, keepdims=True))
    attn = e / e.sum(-1, keepdims=True)
    context = mxq(attn, 2, "e4m3") @ mxq(f64(v), 1, "e4m3")
    context = np.swapaxes(context, 1, 2).reshape(B, -1, D)
    return context, attn

@@ -1,0 +1,299 @@
+import math
+from contextlib import ExitStack
+
+import concourse.mybir as mybir
+from concourse.masks import make_identity
+
+F32 = mybir.dt.float32
+BF16 = mybir.dt.bfloat16
+U32 = mybir.dt.uint32
+U8 = mybir.dt.uint8
+FP8X4 = mybir.dt.float8_e4m3fn_x4
+ADD = mybir.AluOpType.add
+MULT = mybir.AluOpType.mult
+MAX = mybir.AluOpType.max
+EXP = mybir.ActivationFunctionType.Exp
+ALONG_ROW = mybir.AxisListType.X
+
+P = 128
+PACK = 4
+K_PASS = P * PACK
+BATCH, LENGTH = 2, 1024
+PASSES = LENGTH // K_PASS
+BANK = 512
+INV_SCALE = 1.0 / math.sqrt(2.0 * 64)
+FLOPS = 2 * 2 * BATCH * LENGTH * LENGTH * LENGTH
+
+TILES_PER_BATCH = LENGTH // P
+TILES = BATCH * TILES_PER_BATCH
+UNIT_COLS = 2048
+UNIT_WORDS = UNIT_COLS // PACK
+UNIT_ROWS = 256
+K_KIND, Q_KIND, V_KIND = 0, 1, 2
+PARTS = 4
+ROW_UNITS = [(b, kind, part) for b in range(BATCH) for kind in (K_KIND, Q_KIND) for part in range(PARTS)]
+V_UNITS = [(b, V_KIND, part) for b in range(BATCH) for part in range(PARTS)]
+ROW_HEAD = 5
+RAW_RING = 16
+OUT_TILES = 2
+
+
+def tile_multiheadattention_tupe_pb_kernel(tc, q, k, v, pos_bias, out, attn):
+    nc = tc.nc
+    with ExitStack() as ctx:
+        const = ctx.enter_context(tc.tile_pool(name="const", bufs=1))
+        raw_pool = ctx.enter_context(tc.tile_pool(name="raw", bufs=RAW_RING))
+        operands = ctx.enter_context(tc.tile_pool(name="operands", bufs=1))
+        stage = ctx.enter_context(tc.tile_pool(name="stage", bufs=4))
+        soft = ctx.enter_context(tc.tile_pool(name="soft", bufs=2))
+        attn_pool = ctx.enter_context(tc.tile_pool(name="attn", bufs=5))
+        stats = ctx.enter_context(tc.tile_pool(name="stats", bufs=3))
+        out_pool = ctx.enter_context(tc.tile_pool(name="out", bufs=2))
+        psum = ctx.enter_context(tc.psum_pool(name="psum", bufs=2))
+        ctx.enter_context(tc.manual_schedule())
+
+        raw, grouped, codes, scales = {}, {}, {}, {}
+        bias = {}
+
+        def load_unit(unit):
+            b, kind, part = unit
+            raw[unit] = raw_pool.tile([P, UNIT_COLS], BF16, name="raw")
+            if kind == V_KIND:
+                half, g = divmod(part, PASSES)
+                rows = v[b, K_PASS * g : K_PASS * (g + 1), BANK * half : BANK * (half + 1)]
+                nc.sync.dma_start(
+                    out=raw[unit][:].rearrange("p (j d) -> p j d", j=PACK),
+                    in_=rows.rearrange("(j p) d -> p j d", p=P),
+                )
+            else:
+                x = k if kind == K_KIND else q
+                rows = x[b, UNIT_ROWS * part : UNIT_ROWS * (part + 1), :]
+                nc.sync.dma_start(
+                    out=raw[unit][:].rearrange("p (t d) -> p t d", t=2),
+                    in_=rows.rearrange("(t p) d -> p t d", p=P),
+                )
+
+        def load_bias(pair):
+            bias[pair] = const.tile([P, 2, LENGTH], BF16, name="bias%d" % pair)
+            rows = pos_bias[2 * P * pair : 2 * P * (pair + 1), :]
+            nc.sync.dma_start(out=bias[pair][:], in_=rows.rearrange("(t p) c -> p t c", p=P))
+
+        def flip_rows(unit):
+            words = raw[unit][:].bitcast(F32)
+            flipped = {}
+            for g in range(PASSES):
+                flipped[g] = psum.tile([P, 2, UNIT_ROWS], F32, name="flipped")
+                for t in range(2):
+                    for h in range(2):
+                        first = BANK * t + 256 * g + P * h
+                        nc.tensor.transpose(
+                            flipped[g][:, h, P * t : P * (t + 1)], words[:, first : first + P], ident[:]
+                        )
+            return flipped
+
+        def group_rows(unit, flipped, copies):
+            grouped[unit] = stage.tile([P, UNIT_COLS], BF16, name="grouped", align_bytes=64)
+            grouped_words = grouped[unit][:].bitcast(F32)
+            for g in range(PASSES):
+                copies[g](
+                    out=grouped_words[:, BANK * g : BANK * (g + 1)].rearrange("p (r h) -> p r h", h=2),
+                    in_=flipped[g][:].rearrange("p h r -> p r h"),
+                )
+
+        def group_v(unit):
+            grouped[unit] = stage.tile([P, UNIT_COLS], BF16, name="grouped", align_bytes=64)
+            nc.vector.tensor_copy(
+                out=grouped[unit][:].rearrange("p (c i j) -> p c j i", i=4, j=PACK),
+                in_=raw[unit][:].rearrange("p (j c i) -> p c j i", j=PACK, i=4),
+            )
+
+        def quantise_unit(unit):
+            codes[unit] = operands.tile([P, UNIT_WORDS], U32, name="codes%d%d%d" % unit, align_bytes=64)
+            scales[unit] = operands.tile([P, UNIT_WORDS], U8, name="scales%d%d%d" % unit, align_bytes=64)
+            nc.vector.quantize_mx(
+                out=codes[unit][:].bitcast(FP8X4), scales=scales[unit][:], in_=grouped[unit][:]
+            )
+
+        score_banks, summed, row_max, shift, row_sum, inv_sum = {}, {}, {}, {}, {}, {}
+        expd, attn_sb, attn_t, attn_grouped, attn_codes, attn_scales = {}, {}, {}, {}, {}, {}
+        context_banks, out_sb = {}, {}
+
+        def score_matmuls(i):
+            b, m = divmod(i, TILES_PER_BATCH)
+            mine_unit = (b, Q_KIND, m // 2)
+            score_banks[i] = []
+            for half in range(2):
+                bank = psum.tile([P, BANK], F32, name="scores")
+                score_banks[i].append(bank)
+                for part in (2 * half, 2 * half + 1):
+                    keys_unit = (b, K_KIND, part)
+                    for g in range(PASSES):
+                        mine = slice(UNIT_ROWS * g + P * (m % 2), UNIT_ROWS * g + P * (m % 2) + P)
+                        keys = slice(UNIT_ROWS * g, UNIT_ROWS * (g + 1))
+                        nc.tensor.matmul_mx(
+                            out=bank[:, UNIT_ROWS * (part % 2) : UNIT_ROWS * (part % 2 + 1)],
+                            lhsT=codes[mine_unit][:, mine].bitcast(FP8X4),
+                            lhsT_scale=scales[mine_unit][:, mine],
+                            rhs=codes[keys_unit][:, keys].bitcast(FP8X4),
+                            rhs_scale=scales[keys_unit][:, keys],
+                            start=(g == 0),
+                            stop=(g == PASSES - 1),
+                        )
+
+        def add_bias(i, half):
+            m = i % TILES_PER_BATCH
+            if half == 0:
+                summed[i] = soft.tile([P, LENGTH], F32, name="summed")
+            cols = slice(BANK * half, BANK * (half + 1))
+            nc.vector.tensor_tensor(
+                out=summed[i][:, cols], in0=score_banks[i][half][:], in1=bias[m // 2][:, m % 2, cols], op=ADD
+            )
+
+        def find_shift(i):
+            row_max[i] = stats.tile([P, 1], F32, name="row_max")
+            shift[i] = stats.tile([P, 1], F32, name="shift")
+            nc.vector.tensor_reduce(out=row_max[i][:], in_=summed[i][:], axis=ALONG_ROW, op=MAX)
+            nc.vector.tensor_scalar(out=shift[i][:], in0=row_max[i][:], scalar1=-INV_SCALE, scalar2=None, op0=MULT)
+
+        def exponentials(i):
+            expd[i] = soft.tile([P, LENGTH], F32, name="expd")
+            row_sum[i] = stats.tile([P, 1], F32, name="row_sum")
+            nc.scalar.activation(
+                out=expd[i][:], in_=summed[i][:], func=EXP, bias=shift[i][:], scale=INV_SCALE, accum_out=row_sum[i][:]
+            )
+
+        def invert_sum(i):
+            inv_sum[i] = stats.tile([P, 1], F32, name="inv_sum")
+            nc.vector.reciprocal(out=inv_sum[i][:], in_=row_sum[i][:])
+
+        def normalise(i):
+            b, m = divmod(i, TILES_PER_BATCH)
+            attn_sb[i] = attn_pool.tile([P, LENGTH], F32, name="attn_sb")
+            nc.vector.tensor_scalar(
+                out=attn_sb[i][:], in0=expd[i][:], scalar1=inv_sum[i][:], scalar2=None, op0=MULT
+            )
+            nc.sync.dma_start(out=attn[b, P * m : P * (m + 1), :], in_=attn_sb[i][:])
+
+        def transpose_attn(i):
+            attn_t[i] = []
+            for g in range(PASSES):
+                bank = psum.tile([P, PACK, P], F32, name="attn_t")
+                attn_t[i].append(bank)
+                for j in range(PACK):
+                    first = K_PASS * g + P * j
+                    nc.tensor.transpose(bank[:, j, :], attn_sb[i][:, first : first + P], ident[:])
+
+        def group_attn(i, copies):
+            attn_grouped[i] = stage.tile([P, PASSES, P, PACK], BF16, name="attn_grouped", align_bytes=64)
+            for g in range(PASSES):
+                copies[g](out=attn_grouped[i][:, g], in_=attn_t[i][g][:].rearrange("p j s -> p s j"))
+
+        def quantise_attn(i):
+            attn_codes[i] = stage.tile([P, PASSES * P], U32, name="attn_codes", align_bytes=64)
+            attn_scales[i] = stage.tile([P, PASSES * P], U8, name="attn_scales", align_bytes=64)
+            nc.vector.quantize_mx(
+                out=attn_codes[i][:].bitcast(FP8X4),
+                scales=attn_scales[i][:],
+                in_=attn_grouped[i][:].rearrange("p g s j -> p (g s j)"),
+            )
+
+        def context_matmuls(i):
+            b = i // TILES_PER_BATCH
+            context_banks[i] = []
+            for half in range(2):
+                bank = psum.tile([P, 4, P], F32, name="context")
+                context_banks[i].append(bank)
+                for f in range(4):
+                    for g in range(PASSES):
+                        v_unit = (b, V_KIND, PASSES * half + g)
+                        feats = slice(P * f, P * (f + 1))
+                        mine = slice(P * g, P * (g + 1))
+                        nc.tensor.matmul_mx(
+                            out=bank[:, f, :],
+                            lhsT=codes[v_unit][:, feats].bitcast(FP8X4),
+                            lhsT_scale=scales[v_unit][:, feats],
+                            rhs=attn_codes[i][:, mine].bitcast(FP8X4),
+                            rhs_scale=attn_scales[i][:, mine],
+                            start=(g == 0),
+                            stop=(g == PASSES - 1),
+                        )
+
+        def copy_context(i, half, copy):
+            first, place = i - i % OUT_TILES, i % OUT_TILES
+            if place == 0 and half == 0:
+                out_sb[first] = out_pool.tile([P, 8, OUT_TILES * P], F32, name="out_sb")
+            copy(
+                out=out_sb[first][:, 4 * half : 4 * (half + 1), P * place : P * (place + 1)],
+                in_=context_banks[i][half][:],
+            )
+
+        def store_context(i):
+            b, m = divmod(i, TILES_PER_BATCH)
+            first, place = i - i % OUT_TILES, i % OUT_TILES
+            if place == OUT_TILES - 1:
+                cols = slice(P * (m - place), P * (m + 1))
+                nc.sync.dma_start(out=out[b].rearrange("(f p) s -> p f s", p=P)[:, :, cols], in_=out_sb[first][:])
+
+        on_scalar, on_vector = nc.scalar.copy, nc.vector.tensor_copy
+
+        ident = const.tile([P, P], F32, name="ident")
+        make_identity(nc, ident[:])
+        load_order = ROW_UNITS[:ROW_HEAD]
+        for step in range(len(ROW_UNITS) - ROW_HEAD):
+            load_order += ROW_UNITS[ROW_HEAD + step : ROW_HEAD + step + 1] + V_UNITS[step : step + 1]
+        for place in range(RAW_RING):
+            load_unit(load_order[place])
+            pair, odd = divmod(place - (ROW_HEAD - 1), 2)
+            if 0 <= pair < TILES_PER_BATCH // 2 and odd == 0:
+                load_bias(pair)
+
+        def load_behind(unit):
+            place = load_order.index(unit) + RAW_RING
+            if place < len(load_order):
+                load_unit(load_order[place])
+
+        for n in range(ROW_HEAD):
+            group_rows(ROW_UNITS[n], flip_rows(ROW_UNITS[n]), (on_scalar, on_vector))
+            load_behind(ROW_UNITS[n])
+            if n > 0:
+                quantise_unit(ROW_UNITS[n - 1])
+        quantise_unit(ROW_UNITS[ROW_HEAD - 1])
+        score_matmuls(0)
+
+        for step in range(TILES + 4):
+            row_units = ROW_UNITS[ROW_HEAD + step : ROW_HEAD + step + 1]
+            v_units = V_UNITS[step : step + 1]
+            for unit in row_units:
+                group_rows(unit, flip_rows(unit), (on_scalar, on_scalar))
+                load_behind(unit)
+            if 0 <= step - 4:
+                context_matmuls(step - 4)
+            if 0 <= step - 2 < TILES:
+                group_attn(step - 2, (on_scalar, on_scalar))
+            if step < TILES:
+                add_bias(step, 0)
+            if 0 <= step - 1 < TILES:
+                invert_sum(step - 1)
+            if step < TILES:
+                add_bias(step, 1)
+                find_shift(step)
+            for unit in row_units:
+                quantise_unit(unit)
+            if step + 1 < TILES:
+                score_matmuls(step + 1)
+            if 0 <= step - 1 < TILES:
+                normalise(step - 1)
+                transpose_attn(step - 1)
+            for unit in v_units:
+                group_v(unit)
+                load_behind(unit)
+            if 0 <= step - 2 < TILES:
+                quantise_attn(step - 2)
+            if 0 <= step - 4:
+                copy_context(step - 4, 0, on_scalar)
+                copy_context(step - 4, 1, on_scalar)
+                store_context(step - 4)
+            if step < TILES:
+                exponentials(step)
+            for unit in v_units:
+                quantise_unit(unit)

@@ -31,11 +31,14 @@ UNIT_WORDS = UNIT_COLS // PACK
 UNIT_ROWS = 256
 K_KIND, Q_KIND, V_KIND = 0, 1, 2
 PARTS = 4
-ROW_UNITS = [(b, kind, part) for b in range(BATCH) for kind in (K_KIND, Q_KIND) for part in range(PARTS)]
+ROW_ORDER = [(Q_KIND, 0)] + [(K_KIND, part) for part in range(PARTS)] + [(Q_KIND, part) for part in range(1, PARTS)]
+ROW_UNITS = [(b, kind, part) for b in range(BATCH) for kind, part in ROW_ORDER]
 V_UNITS = [(b, V_KIND, part) for b in range(BATCH) for part in range(PARTS)]
-ROW_HEAD = 5
+ROW_HEAD = 1 + PARTS
+V_FIRST = 2
 RAW_RING = 16
 OUT_TILES = 2
+PSUM_TAGS = ("flipped", "scores", "attn_t", "context")
 
 
 def tile_multiheadattention_tupe_pb_kernel(tc, q, k, v, pos_bias, out, attn):
@@ -48,7 +51,7 @@ def tile_multiheadattention_tupe_pb_kernel(tc, q, k, v, pos_bias, out, attn):
         soft = ctx.enter_context(tc.tile_pool(name="soft", bufs=2))
         attn_pool = ctx.enter_context(tc.tile_pool(name="attn", bufs=5))
         stats = ctx.enter_context(tc.tile_pool(name="stats", bufs=3))
-        out_pool = ctx.enter_context(tc.tile_pool(name="out", bufs=2))
+        out_pool = ctx.enter_context(tc.tile_pool(name="out", bufs=4))
         psum = ctx.enter_context(tc.psum_pool(name="psum", bufs=2))
         ctx.enter_context(tc.manual_schedule())
 
@@ -78,11 +81,11 @@ def tile_multiheadattention_tupe_pb_kernel(tc, q, k, v, pos_bias, out, attn):
             rows = pos_bias[2 * P * pair : 2 * P * (pair + 1), :]
             nc.sync.dma_start(out=bias[pair][:], in_=rows.rearrange("(t p) c -> p t c", p=P))
 
-        def flip_rows(unit):
+        def flip_rows(unit, banks):
             words = raw[unit][:].bitcast(F32)
             flipped = {}
             for g in range(PASSES):
-                flipped[g] = psum.tile([P, 2, UNIT_ROWS], F32, name="flipped")
+                flipped[g] = psum.tile([P, 2, UNIT_ROWS], F32, name="flipped", tag=banks)
                 for t in range(2):
                     for h in range(2):
                         first = BANK * t + 256 * g + P * h
@@ -169,8 +172,8 @@ def tile_multiheadattention_tupe_pb_kernel(tc, q, k, v, pos_bias, out, attn):
         def normalise(i):
             b, m = divmod(i, TILES_PER_BATCH)
             attn_sb[i] = attn_pool.tile([P, LENGTH], F32, name="attn_sb")
-            nc.vector.tensor_scalar(
-                out=attn_sb[i][:], in0=expd[i][:], scalar1=inv_sum[i][:], scalar2=None, op0=MULT
+            nc.gpsimd.tensor_scalar(
+                out=attn_sb[i][:], in0=expd[i][:], scalar1=inv_sum[i][:], scalar2=0.0, op0=MULT, op1=ADD
             )
             nc.sync.dma_start(out=attn[b, P * m : P * (m + 1), :], in_=attn_sb[i][:])
 
@@ -219,28 +222,28 @@ def tile_multiheadattention_tupe_pb_kernel(tc, q, k, v, pos_bias, out, attn):
                         )
 
         def copy_context(i, half, copy):
-            first, place = i - i % OUT_TILES, i % OUT_TILES
-            if place == 0 and half == 0:
-                out_sb[first] = out_pool.tile([P, 8, OUT_TILES * P], F32, name="out_sb")
-            copy(
-                out=out_sb[first][:, 4 * half : 4 * (half + 1), P * place : P * (place + 1)],
-                in_=context_banks[i][half][:],
-            )
-
-        def store_context(i):
             b, m = divmod(i, TILES_PER_BATCH)
             first, place = i - i % OUT_TILES, i % OUT_TILES
+            if place == 0:
+                out_sb[first, half] = out_pool.tile([P, 4, OUT_TILES * P], F32, name="out_sb")
+            copy(out=out_sb[first, half][:, :, P * place : P * (place + 1)], in_=context_banks[i][half][:])
             if place == OUT_TILES - 1:
-                cols = slice(P * (m - place), P * (m + 1))
-                nc.sync.dma_start(out=out[b].rearrange("(f p) s -> p f s", p=P)[:, :, cols], in_=out_sb[first][:])
+                rows = out[b, BANK * half : BANK * (half + 1), P * (m - place) : P * (m + 1)]
+                nc.sync.dma_start(out=rows.rearrange("(f p) s -> p f s", p=P), in_=out_sb[first, half][:])
 
         on_scalar, on_vector = nc.scalar.copy, nc.vector.tensor_copy
 
         ident = const.tile([P, P], F32, name="ident")
         make_identity(nc, ident[:])
+        def units_of_step(step):
+            row_units = ROW_UNITS[ROW_HEAD + step : ROW_HEAD + step + 1]
+            v_units = V_UNITS[:V_FIRST] if step == 0 else V_UNITS[V_FIRST + step - 1 : V_FIRST + step]
+            return row_units, v_units
+
         load_order = ROW_UNITS[:ROW_HEAD]
-        for step in range(len(ROW_UNITS) - ROW_HEAD):
-            load_order += ROW_UNITS[ROW_HEAD + step : ROW_HEAD + step + 1] + V_UNITS[step : step + 1]
+        for step in range(TILES):
+            row_units, v_units = units_of_step(step)
+            load_order += row_units + v_units
         for place in range(RAW_RING):
             load_unit(load_order[place])
             pair, odd = divmod(place - (ROW_HEAD - 1), 2)
@@ -253,27 +256,28 @@ def tile_multiheadattention_tupe_pb_kernel(tc, q, k, v, pos_bias, out, attn):
                 load_unit(load_order[place])
 
         for n in range(ROW_HEAD):
-            group_rows(ROW_UNITS[n], flip_rows(ROW_UNITS[n]), (on_scalar, on_vector))
+            group_rows(ROW_UNITS[n], flip_rows(ROW_UNITS[n], PSUM_TAGS[n % len(PSUM_TAGS)]), (on_scalar, on_vector))
             load_behind(ROW_UNITS[n])
             if n > 0:
                 quantise_unit(ROW_UNITS[n - 1])
         quantise_unit(ROW_UNITS[ROW_HEAD - 1])
         score_matmuls(0)
 
-        for step in range(TILES + 4):
-            row_units = ROW_UNITS[ROW_HEAD + step : ROW_HEAD + step + 1]
-            v_units = V_UNITS[step : step + 1]
+        for step in range(TILES + 3):
+            row_units, v_units = units_of_step(step)
+            spare = on_scalar if v_units else on_vector
             for unit in row_units:
-                group_rows(unit, flip_rows(unit), (on_scalar, on_scalar))
+                group_rows(unit, flip_rows(unit, "flipped"), (on_scalar, on_scalar))
                 load_behind(unit)
-            if 0 <= step - 4:
-                context_matmuls(step - 4)
+            if 0 <= step - 3:
+                context_matmuls(step - 3)
             if 0 <= step - 2 < TILES:
                 group_attn(step - 2, (on_scalar, on_scalar))
             if step < TILES:
                 add_bias(step, 0)
             if 0 <= step - 1 < TILES:
                 invert_sum(step - 1)
+                normalise(step - 1)
             if step < TILES:
                 add_bias(step, 1)
                 find_shift(step)
@@ -282,17 +286,15 @@ def tile_multiheadattention_tupe_pb_kernel(tc, q, k, v, pos_bias, out, attn):
             if step + 1 < TILES:
                 score_matmuls(step + 1)
             if 0 <= step - 1 < TILES:
-                normalise(step - 1)
                 transpose_attn(step - 1)
             for unit in v_units:
                 group_v(unit)
                 load_behind(unit)
             if 0 <= step - 2 < TILES:
                 quantise_attn(step - 2)
-            if 0 <= step - 4:
-                copy_context(step - 4, 0, on_scalar)
-                copy_context(step - 4, 1, on_scalar)
-                store_context(step - 4)
+            if 0 <= step - 3:
+                copy_context(step - 3, 0, on_scalar)
+                copy_context(step - 3, 1, spare)
             if step < TILES:
                 exponentials(step)
             for unit in v_units:

@@ -53,7 +53,6 @@ def tile_multiheadattention_tupe_pb_kernel(tc, q, k, v, pos_bias, out, attn):
         stats = ctx.enter_context(tc.tile_pool(name="stats", bufs=3))
         out_pool = ctx.enter_context(tc.tile_pool(name="out", bufs=4))
         psum = ctx.enter_context(tc.psum_pool(name="psum", bufs=2))
-        ctx.enter_context(tc.manual_schedule())
 
         raw, grouped, codes, scales = {}, {}, {}, {}
         bias = {}

@@ -35,7 +35,7 @@ ROW_ORDER = [(Q_KIND, 0)] + [(K_KIND, part) for part in range(PARTS)] + [(Q_KIND
 ROW_UNITS = [(b, kind, part) for b in range(BATCH) for kind, part in ROW_ORDER]
 V_UNITS = [(b, V_KIND, part) for b in range(BATCH) for part in range(PARTS)]
 ROW_HEAD = 1 + PARTS
-V_FIRST = 2
+V_STEP = 6
 RAW_RING = 16
 OUT_TILES = 2
 PSUM_TAGS = ("flipped", "scores", "attn_t", "context")
@@ -53,6 +53,7 @@ def tile_multiheadattention_tupe_pb_kernel(tc, q, k, v, pos_bias, out, attn):
         stats = ctx.enter_context(tc.tile_pool(name="stats", bufs=3))
         out_pool = ctx.enter_context(tc.tile_pool(name="out", bufs=4))
         psum = ctx.enter_context(tc.psum_pool(name="psum", bufs=2))
+        ctx.enter_context(tc.manual_schedule())
 
         raw, grouped, codes, scales = {}, {}, {}, {}
         bias = {}
@@ -102,9 +103,9 @@ def tile_multiheadattention_tupe_pb_kernel(tc, q, k, v, pos_bias, out, attn):
                     in_=flipped[g][:].rearrange("p h r -> p r h"),
                 )
 
-        def group_v(unit):
+        def group_v(unit, copy):
             grouped[unit] = stage.tile([P, UNIT_COLS], BF16, name="grouped", align_bytes=64)
-            nc.vector.tensor_copy(
+            copy(
                 out=grouped[unit][:].rearrange("p (c i j) -> p c j i", i=4, j=PACK),
                 in_=raw[unit][:].rearrange("p (j c i) -> p c j i", j=PACK, i=4),
             )
@@ -142,14 +143,14 @@ def tile_multiheadattention_tupe_pb_kernel(tc, q, k, v, pos_bias, out, attn):
                             stop=(g == PASSES - 1),
                         )
 
-        def add_bias(i, half):
+        def add_bias(i):
             m = i % TILES_PER_BATCH
-            if half == 0:
-                summed[i] = soft.tile([P, LENGTH], F32, name="summed")
-            cols = slice(BANK * half, BANK * (half + 1))
-            nc.vector.tensor_tensor(
-                out=summed[i][:, cols], in0=score_banks[i][half][:], in1=bias[m // 2][:, m % 2, cols], op=ADD
-            )
+            summed[i] = soft.tile([P, LENGTH], F32, name="summed")
+            for half in range(2):
+                cols = slice(BANK * half, BANK * (half + 1))
+                nc.vector.tensor_tensor(
+                    out=summed[i][:, cols], in0=score_banks[i][half][:], in1=bias[m // 2][:, m % 2, cols], op=ADD
+                )
 
         def find_shift(i):
             row_max[i] = stats.tile([P, 1], F32, name="row_max")
@@ -158,7 +159,7 @@ def tile_multiheadattention_tupe_pb_kernel(tc, q, k, v, pos_bias, out, attn):
             nc.vector.tensor_scalar(out=shift[i][:], in0=row_max[i][:], scalar1=-INV_SCALE, scalar2=None, op0=MULT)
 
         def exponentials(i):
-            expd[i] = soft.tile([P, LENGTH], F32, name="expd")
+            expd[i] = soft.tile([P, LENGTH], F32, name="expd", bufs=3)
             row_sum[i] = stats.tile([P, 1], F32, name="row_sum")
             nc.scalar.activation(
                 out=expd[i][:], in_=summed[i][:], func=EXP, bias=shift[i][:], scale=INV_SCALE, accum_out=row_sum[i][:]
@@ -185,10 +186,10 @@ def tile_multiheadattention_tupe_pb_kernel(tc, q, k, v, pos_bias, out, attn):
                     first = K_PASS * g + P * j
                     nc.tensor.transpose(bank[:, j, :], attn_sb[i][:, first : first + P], ident[:])
 
-        def group_attn(i, copies):
+        def group_attn(i):
             attn_grouped[i] = stage.tile([P, PASSES, P, PACK], BF16, name="attn_grouped", align_bytes=64)
             for g in range(PASSES):
-                copies[g](out=attn_grouped[i][:, g], in_=attn_t[i][g][:].rearrange("p j s -> p s j"))
+                nc.scalar.copy(out=attn_grouped[i][:, g], in_=attn_t[i][g][:].rearrange("p j s -> p s j"))
 
         def quantise_attn(i):
             attn_codes[i] = stage.tile([P, PASSES * P], U32, name="attn_codes", align_bytes=64)
@@ -236,7 +237,7 @@ def tile_multiheadattention_tupe_pb_kernel(tc, q, k, v, pos_bias, out, attn):
         make_identity(nc, ident[:])
         def units_of_step(step):
             row_units = ROW_UNITS[ROW_HEAD + step : ROW_HEAD + step + 1]
-            v_units = V_UNITS[:V_FIRST] if step == 0 else V_UNITS[V_FIRST + step - 1 : V_FIRST + step]
+            v_units = [(b, kind, part) for b, kind, part in V_UNITS if V_STEP * b + part == step]
             return row_units, v_units
 
         load_order = ROW_UNITS[:ROW_HEAD]
@@ -262,39 +263,40 @@ def tile_multiheadattention_tupe_pb_kernel(tc, q, k, v, pos_bias, out, attn):
         quantise_unit(ROW_UNITS[ROW_HEAD - 1])
         score_matmuls(0)
 
-        for step in range(TILES + 3):
+        def live(i):
+            return 0 <= i < TILES
+
+        for step in range(TILES + 4):
             row_units, v_units = units_of_step(step)
-            spare = on_scalar if v_units else on_vector
             for unit in row_units:
                 group_rows(unit, flip_rows(unit, "flipped"), (on_scalar, on_scalar))
                 load_behind(unit)
-            if 0 <= step - 3:
-                context_matmuls(step - 3)
-            if 0 <= step - 2 < TILES:
-                group_attn(step - 2, (on_scalar, on_scalar))
-            if step < TILES:
-                add_bias(step, 0)
-            if 0 <= step - 1 < TILES:
-                invert_sum(step - 1)
-                normalise(step - 1)
-            if step < TILES:
-                add_bias(step, 1)
+            if live(step - 4):
+                context_matmuls(step - 4)
+            if live(step - 3):
+                group_attn(step - 3)
+            if live(step):
+                add_bias(step)
                 find_shift(step)
             for unit in row_units:
                 quantise_unit(unit)
-            if step + 1 < TILES:
+            if live(step + 1):
                 score_matmuls(step + 1)
-            if 0 <= step - 1 < TILES:
-                transpose_attn(step - 1)
-            for unit in v_units:
-                group_v(unit)
-                load_behind(unit)
-            if 0 <= step - 2 < TILES:
-                quantise_attn(step - 2)
-            if 0 <= step - 3:
-                copy_context(step - 3, 0, on_scalar)
-                copy_context(step - 3, 1, spare)
-            if step < TILES:
+            if live(step - 2):
+                transpose_attn(step - 2)
+            for b, kind, part in v_units:
+                group_v((b, kind, part), on_scalar if b == 0 and part % 2 == 1 else on_vector)
+                load_behind((b, kind, part))
+            if live(step - 3):
+                quantise_attn(step - 3)
+            if live(step - 4):
+                copy_context(step - 4, 0, on_scalar)
+            if live(step):
                 exponentials(step)
             for unit in v_units:
                 quantise_unit(unit)
+            if live(step - 1):
+                invert_sum(step - 1)
+                normalise(step - 1)
+            if live(step - 4):
+                copy_context(step - 4, 1, on_scalar if v_units else on_vector)

@@ -117,7 +117,7 @@ def tile_multiheadattention_tupe_pb_kernel(tc, q, k, v, pos_bias, out, attn):
                 out=codes[unit][:].bitcast(FP8X4), scales=scales[unit][:], in_=grouped[unit][:]
             )
 
-        score_banks, summed, row_max, shift, row_sum, inv_sum = {}, {}, {}, {}, {}, {}
+        score_banks, summed, half_max, shift, row_sum, inv_sum = {}, {}, {}, {}, {}, {}
         expd, attn_sb, attn_t, attn_grouped, attn_codes, attn_scales = {}, {}, {}, {}, {}, {}
         context_banks, out_sb = {}, {}
 
@@ -152,11 +152,18 @@ def tile_multiheadattention_tupe_pb_kernel(tc, q, k, v, pos_bias, out, attn):
                     out=summed[i][:, cols], in0=score_banks[i][half][:], in1=bias[m // 2][:, m % 2, cols], op=ADD
                 )
 
+        def find_maxima(i):
+            half_max[i] = []
+            for half in range(2):
+                cols = slice(BANK * half, BANK * (half + 1))
+                half_max[i].append(stats.tile([P, 1], F32, name="half_max%d" % half))
+                nc.vector.tensor_reduce(out=half_max[i][half][:], in_=summed[i][:, cols], axis=ALONG_ROW, op=MAX)
+
         def find_shift(i):
-            row_max[i] = stats.tile([P, 1], F32, name="row_max")
             shift[i] = stats.tile([P, 1], F32, name="shift")
-            nc.vector.tensor_reduce(out=row_max[i][:], in_=summed[i][:], axis=ALONG_ROW, op=MAX)
-            nc.vector.tensor_scalar(out=shift[i][:], in0=row_max[i][:], scalar1=-INV_SCALE, scalar2=None, op0=MULT)
+            nc.vector.tensor_scalar(
+                out=shift[i][:], in0=half_max[i][0][:], scalar1=half_max[i][1][:], scalar2=-INV_SCALE, op0=MAX, op1=MULT
+            )
 
         def exponentials(i):
             expd[i] = soft.tile([P, LENGTH], F32, name="expd", bufs=3)
@@ -277,9 +284,13 @@ def tile_multiheadattention_tupe_pb_kernel(tc, q, k, v, pos_bias, out, attn):
                 group_attn(step - 3)
             if live(step):
                 add_bias(step)
-                find_shift(step)
+                find_maxima(step)
             for unit in row_units:
                 quantise_unit(unit)
+            if live(step - 3):
+                quantise_attn(step - 3)
+            if live(step):
+                find_shift(step)
             if live(step + 1):
                 score_matmuls(step + 1)
             if live(step - 2):
@@ -287,8 +298,6 @@ def tile_multiheadattention_tupe_pb_kernel(tc, q, k, v, pos_bias, out, attn):
             for b, kind, part in v_units:
                 group_v((b, kind, part), on_scalar if b == 0 and part % 2 == 1 else on_vector)
                 load_behind((b, kind, part))
-            if live(step - 3):
-                quantise_attn(step - 3)
             if live(step - 4):
                 copy_context(step - 4, 0, on_scalar)
             if live(step):

@@ -36,7 +36,13 @@ ROW_UNITS = [(b, kind, part) for b in range(BATCH) for kind, part in ROW_ORDER]
 V_UNITS = [(b, V_KIND, part) for b in range(BATCH) for part in range(PARTS)]
 ROW_HEAD = 1 + PARTS
 V_STEP = 6
-RAW_RING = 16
+V_PLAN = {0: [(0, 0, "V", 0, 512)], 1: [(0, 1, "S", 0, 512)], 2: [(0, 2, "V", 0, 512)], 3: [(0, 3, "S", 0, 512)], 6: [(1, 0, "S", 0, 64), (1, 0, "V", 64, 512)], 7: [(1, 1, "S", 0, 64), (1, 1, "V", 64, 512)], 8: [(1, 2, "S", 0, 64), (1, 2, "V", 64, 512)], 9: [(1, 3, "S", 0, 64), (1, 3, "V", 64, 512)]}
+V_QUANT = {3: [(0, 3)]}
+V_LATE = {1: [(0, 0)], 2: [(0, 1)], 3: [(0, 2)], 7: [(1, 0)], 8: [(1, 1)], 9: [(1, 2)], 10: [(1, 3)]}
+V_LOADS = {0: [(0, 0)], 1: [(0, 1)], 2: [(0, 2)], 3: [(0, 3)], 6: [(1, 0)], 7: [(1, 1)], 8: [(1, 2)], 9: [(1, 3)]}
+ROW_STEPS = {n: [5 + n] for n in range(11)}
+CTX_V = (4, 5, 10, 11, 12, 13, 14, 15)
+RAW_RING = 15
 OUT_TILES = 2
 PSUM_TAGS = ("flipped", "scores", "attn_t", "context")
 
@@ -58,9 +64,10 @@ def tile_multiheadattention_tupe_pb_kernel(tc, q, k, v, pos_bias, out, attn):
         raw, grouped, codes, scales = {}, {}, {}, {}
         bias = {}
 
-        def load_unit(unit):
+        def load_unit(unit, tiles=slice(0, 2)):
             b, kind, part = unit
-            raw[unit] = raw_pool.tile([P, UNIT_COLS], BF16, name="raw")
+            if unit not in raw:
+                raw[unit] = raw_pool.tile([P, UNIT_COLS], BF16, name="raw")
             if kind == V_KIND:
                 half, g = divmod(part, PASSES)
                 rows = v[b, K_PASS * g : K_PASS * (g + 1), BANK * half : BANK * (half + 1)]
@@ -72,8 +79,8 @@ def tile_multiheadattention_tupe_pb_kernel(tc, q, k, v, pos_bias, out, attn):
                 x = k if kind == K_KIND else q
                 rows = x[b, UNIT_ROWS * part : UNIT_ROWS * (part + 1), :]
                 nc.sync.dma_start(
-                    out=raw[unit][:].rearrange("p (t d) -> p t d", t=2),
-                    in_=rows.rearrange("(t p) d -> p t d", p=P),
+                    out=raw[unit][:].rearrange("p (t d) -> p t d", t=2)[:, tiles],
+                    in_=rows.rearrange("(t p) d -> p t d", p=P)[:, tiles],
                 )
 
         def load_bias(pair):
@@ -81,11 +88,10 @@ def tile_multiheadattention_tupe_pb_kernel(tc, q, k, v, pos_bias, out, attn):
             rows = pos_bias[2 * P * pair : 2 * P * (pair + 1), :]
             nc.sync.dma_start(out=bias[pair][:], in_=rows.rearrange("(t p) c -> p t c", p=P))
 
-        def flip_rows(unit, banks):
+        def flip_k(unit, banks):
             words = raw[unit][:].bitcast(F32)
-            flipped = {}
+            flipped = [psum.tile([P, 2, UNIT_ROWS], F32, name="flipped", tag=banks) for g in range(PASSES)]
             for g in range(PASSES):
-                flipped[g] = psum.tile([P, 2, UNIT_ROWS], F32, name="flipped", tag=banks)
                 for t in range(2):
                     for h in range(2):
                         first = BANK * t + 256 * g + P * h
@@ -94,7 +100,7 @@ def tile_multiheadattention_tupe_pb_kernel(tc, q, k, v, pos_bias, out, attn):
                         )
             return flipped
 
-        def group_rows(unit, flipped, copies):
+        def group_k(unit, flipped, copies):
             grouped[unit] = stage.tile([P, UNIT_COLS], BF16, name="grouped", align_bytes=64)
             grouped_words = grouped[unit][:].bitcast(F32)
             for g in range(PASSES):
@@ -103,18 +109,48 @@ def tile_multiheadattention_tupe_pb_kernel(tc, q, k, v, pos_bias, out, attn):
                     in_=flipped[g][:].rearrange("p h r -> p r h"),
                 )
 
-        def group_v(unit, copy):
-            grouped[unit] = stage.tile([P, UNIT_COLS], BF16, name="grouped", align_bytes=64)
+        def flip_q(unit, t, banks):
+            words = raw[unit][:].bitcast(F32)
+            flipped = psum.tile([P, PASSES, 2, P], F32, name="flipped", tag=banks)
+            for g in range(PASSES):
+                for h in range(2):
+                    first = BANK * t + 256 * g + P * h
+                    nc.tensor.transpose(flipped[:, g, h, :], words[:, first : first + P], ident[:])
+            return flipped
+
+        def group_q(unit, t, flipped, copy):
+            if unit not in grouped:
+                grouped[unit] = stage.tile([P, UNIT_COLS], BF16, name="grouped", align_bytes=64)
             copy(
-                out=grouped[unit][:].rearrange("p (c i j) -> p c j i", i=4, j=PACK),
-                in_=raw[unit][:].rearrange("p (j c i) -> p c j i", j=PACK, i=4),
+                out=grouped[unit][:].bitcast(F32)[:, BANK * t : BANK * (t + 1)].rearrange("p (g r h) -> p g r h", g=PASSES, h=2),
+                in_=flipped[:].rearrange("p g h r -> p g r h"),
             )
 
-        def quantise_unit(unit):
-            codes[unit] = operands.tile([P, UNIT_WORDS], U32, name="codes%d%d%d" % unit, align_bytes=64)
-            scales[unit] = operands.tile([P, UNIT_WORDS], U8, name="scales%d%d%d" % unit, align_bytes=64)
+        def prepare_rows(unit, banks, copies):
+            if unit[1] == K_KIND:
+                group_k(unit, flip_k(unit, banks), copies)
+            else:
+                both = [flip_q(unit, t, banks) for t in range(2)]
+                for t in range(2):
+                    group_q(unit, t, both[t], copies[t])
+            load_behind(unit)
+
+        def group_v(unit, copy, first, last):
+            if unit not in grouped:
+                grouped[unit] = stage.tile([P, UNIT_COLS], BF16, name="grouped_v", align_bytes=64, bufs=4)
+            copy(
+                out=grouped[unit][:, PACK * first : PACK * last].rearrange("p (c i j) -> p c j i", i=4, j=PACK),
+                in_=raw[unit][:].rearrange("p (j c i) -> p c j i", j=PACK, i=4)[:, first // 4 : last // 4],
+            )
+
+        def quantise_unit(unit, first=0, last=UNIT_WORDS):
+            if unit not in codes:
+                codes[unit] = operands.tile([P, UNIT_WORDS], U32, name="codes%d%d%d" % unit, align_bytes=64)
+                scales[unit] = operands.tile([P, UNIT_WORDS], U8, name="scales%d%d%d" % unit, align_bytes=64)
             nc.vector.quantize_mx(
-                out=codes[unit][:].bitcast(FP8X4), scales=scales[unit][:], in_=grouped[unit][:]
+                out=codes[unit][:, first:last].bitcast(FP8X4),
+                scales=scales[unit][:, first:last],
+                in_=grouped[unit][:, PACK * first : PACK * last],
             )
 
         score_banks, summed, half_max, shift, row_sum, inv_sum = {}, {}, {}, {}, {}, {}
@@ -131,7 +167,8 @@ def tile_multiheadattention_tupe_pb_kernel(tc, q, k, v, pos_bias, out, attn):
                 for part in (2 * half, 2 * half + 1):
                     keys_unit = (b, K_KIND, part)
                     for g in range(PASSES):
-                        mine = slice(UNIT_ROWS * g + P * (m % 2), UNIT_ROWS * g + P * (m % 2) + P)
+                        first = UNIT_ROWS * (m % 2) + P * g
+                        mine = slice(first, first + P)
                         keys = slice(UNIT_ROWS * g, UNIT_ROWS * (g + 1))
                         nc.tensor.matmul_mx(
                             out=bank[:, UNIT_ROWS * (part % 2) : UNIT_ROWS * (part % 2 + 1)],
@@ -176,27 +213,25 @@ def tile_multiheadattention_tupe_pb_kernel(tc, q, k, v, pos_bias, out, attn):
             inv_sum[i] = stats.tile([P, 1], F32, name="inv_sum")
             nc.vector.reciprocal(out=inv_sum[i][:], in_=row_sum[i][:])
 
-        def normalise(i):
+        def normalise(i, multiply):
             b, m = divmod(i, TILES_PER_BATCH)
             attn_sb[i] = attn_pool.tile([P, LENGTH], F32, name="attn_sb")
-            nc.gpsimd.tensor_scalar(
-                out=attn_sb[i][:], in0=expd[i][:], scalar1=inv_sum[i][:], scalar2=0.0, op0=MULT, op1=ADD
-            )
+            multiply(out=attn_sb[i][:], in0=expd[i][:], scalar1=inv_sum[i][:], scalar2=0.0, op0=MULT, op1=ADD)
             nc.sync.dma_start(out=attn[b, P * m : P * (m + 1), :], in_=attn_sb[i][:])
 
-        def transpose_attn(i):
+        def transpose_attn(i, banks="attn_t"):
             attn_t[i] = []
             for g in range(PASSES):
-                bank = psum.tile([P, PACK, P], F32, name="attn_t")
+                bank = psum.tile([P, PACK, P], F32, name="attn_t", tag=banks)
                 attn_t[i].append(bank)
                 for j in range(PACK):
                     first = K_PASS * g + P * j
                     nc.tensor.transpose(bank[:, j, :], attn_sb[i][:, first : first + P], ident[:])
 
-        def group_attn(i):
+        def group_attn(i, copies):
             attn_grouped[i] = stage.tile([P, PASSES, P, PACK], BF16, name="attn_grouped", align_bytes=64)
             for g in range(PASSES):
-                nc.scalar.copy(out=attn_grouped[i][:, g], in_=attn_t[i][g][:].rearrange("p j s -> p s j"))
+                copies[g](out=attn_grouped[i][:, g], in_=attn_t[i][g][:].rearrange("p j s -> p s j"))
 
         def quantise_attn(i):
             attn_codes[i] = stage.tile([P, PASSES * P], U32, name="attn_codes", align_bytes=64)
@@ -207,11 +242,11 @@ def tile_multiheadattention_tupe_pb_kernel(tc, q, k, v, pos_bias, out, attn):
                 in_=attn_grouped[i][:].rearrange("p g s j -> p (g s j)"),
             )
 
-        def context_matmuls(i):
+        def context_matmuls(i, banks="context"):
             b = i // TILES_PER_BATCH
             context_banks[i] = []
             for half in range(2):
-                bank = psum.tile([P, 4, P], F32, name="context")
+                bank = psum.tile([P, 4, P], F32, name="context", tag=banks)
                 context_banks[i].append(bank)
                 for f in range(4):
                     for g in range(PASSES):
@@ -230,29 +265,43 @@ def tile_multiheadattention_tupe_pb_kernel(tc, q, k, v, pos_bias, out, attn):
 
         def copy_context(i, half, copy):
             b, m = divmod(i, TILES_PER_BATCH)
+            rows = out[b, BANK * half : BANK * (half + 1), :].rearrange("(f p) s -> p f s", p=P)
+            if i >= TILES - 4:
+                if half == 0:
+                    out_sb[i] = raw_pool.tile([P, UNIT_COLS], BF16, name="raw")
+                mine = out_sb[i][:, LENGTH * half : LENGTH * (half + 1)].bitcast(F32).rearrange("p (f s) -> p f s", f=4)
+                copy(out=mine, in_=context_banks[i][half][:])
+                nc.sync.dma_start(out=rows[:, :, P * m : P * (m + 1)], in_=mine)
+                return
             first, place = i - i % OUT_TILES, i % OUT_TILES
             if place == 0:
                 out_sb[first, half] = out_pool.tile([P, 4, OUT_TILES * P], F32, name="out_sb")
             copy(out=out_sb[first, half][:, :, P * place : P * (place + 1)], in_=context_banks[i][half][:])
             if place == OUT_TILES - 1:
-                rows = out[b, BANK * half : BANK * (half + 1), P * (m - place) : P * (m + 1)]
-                nc.sync.dma_start(out=rows.rearrange("(f p) s -> p f s", p=P), in_=out_sb[first, half][:])
+                nc.sync.dma_start(out=rows[:, :, P * (m - place) : P * (m + 1)], in_=out_sb[first, half][:])
 
         on_scalar, on_vector = nc.scalar.copy, nc.vector.tensor_copy
+
+        def on_gpsimd(out, in_):
+            nc.gpsimd.tensor_scalar(out=out, in0=in_, scalar1=1.0, scalar2=0.0, op0=MULT, op1=ADD)
+
 
         ident = const.tile([P, P], F32, name="ident")
         make_identity(nc, ident[:])
         def units_of_step(step):
-            row_units = ROW_UNITS[ROW_HEAD + step : ROW_HEAD + step + 1]
-            v_units = [(b, kind, part) for b, kind, part in V_UNITS if V_STEP * b + part == step]
+            row_units = [ROW_UNITS[n] for n in ROW_STEPS.get(step, [])]
+            v_units = [(b, V_KIND, part) for b, part in V_LOADS.get(step, [])]
             return row_units, v_units
 
         load_order = ROW_UNITS[:ROW_HEAD]
         for step in range(TILES):
             row_units, v_units = units_of_step(step)
             load_order += row_units + v_units
-        for place in range(RAW_RING):
+        load_unit(load_order[0], slice(0, 1))
+        for place in range(1, RAW_RING):
             load_unit(load_order[place])
+            if place == ROW_HEAD - 1:
+                load_unit(load_order[0], slice(1, 2))
             pair, odd = divmod(place - (ROW_HEAD - 1), 2)
             if 0 <= pair < TILES_PER_BATCH // 2 and odd == 0:
                 load_bias(pair)
@@ -262,50 +311,91 @@ def tile_multiheadattention_tupe_pb_kernel(tc, q, k, v, pos_bias, out, attn):
             if place < len(load_order):
                 load_unit(load_order[place])
 
-        for n in range(ROW_HEAD):
-            group_rows(ROW_UNITS[n], flip_rows(ROW_UNITS[n], PSUM_TAGS[n % len(PSUM_TAGS)]), (on_scalar, on_vector))
-            load_behind(ROW_UNITS[n])
-            if n > 0:
-                quantise_unit(ROW_UNITS[n - 1])
-        quantise_unit(ROW_UNITS[ROW_HEAD - 1])
+        on_both = (on_scalar, on_vector)
+        first_q = ROW_UNITS[0]
+        group_q(first_q, 0, flip_q(first_q, 0, "flipped"), on_scalar)
+        prepare_rows(ROW_UNITS[1], "scores", on_both)
+        quantise_unit(first_q, 0, UNIT_WORDS // 2)
+        prepare_rows(ROW_UNITS[2], "attn_t", on_both)
+        quantise_unit(ROW_UNITS[1])
+        prepare_rows(ROW_UNITS[3], "context", on_both)
+        quantise_unit(ROW_UNITS[2])
+        prepare_rows(ROW_UNITS[4], "scores", on_both)
+        quantise_unit(ROW_UNITS[3])
+        quantise_unit(ROW_UNITS[4])
+        group_q(first_q, 1, flip_q(first_q, 1, "flipped"), on_scalar)
         score_matmuls(0)
+        load_behind(first_q)
 
         def live(i):
             return 0 <= i < TILES
 
-        for step in range(TILES + 4):
+        for step in range(TILES):
             row_units, v_units = units_of_step(step)
             for unit in row_units:
-                group_rows(unit, flip_rows(unit, "flipped"), (on_scalar, on_scalar))
-                load_behind(unit)
-            if live(step - 4):
+                prepare_rows(unit, "flipped", (on_scalar, on_scalar))
+            if step >= 4:
                 context_matmuls(step - 4)
-            if live(step - 3):
-                group_attn(step - 3)
+            if step >= 3:
+                group_attn(step - 3, (on_scalar, on_scalar))
             if live(step):
                 add_bias(step)
+                if step == TILES - 1:
+                    invert_sum(step - 1)
+                    normalise(step - 1, nc.gpsimd.tensor_scalar)
+                if step == 0:
+                    quantise_unit(first_q, UNIT_WORDS // 2, UNIT_WORDS)
                 find_maxima(step)
+            if step == TILES - 1:
+                find_shift(step)
             for unit in row_units:
                 quantise_unit(unit)
-            if live(step - 3):
+            for b, part in V_LATE.get(step, []):
+                quantise_unit((b, V_KIND, part))
+            if step >= 3:
                 quantise_attn(step - 3)
-            if live(step):
+            if step < TILES - 1:
                 find_shift(step)
             if live(step + 1):
                 score_matmuls(step + 1)
-            if live(step - 2):
+            if step >= 2:
                 transpose_attn(step - 2)
-            for b, kind, part in v_units:
-                group_v((b, kind, part), on_scalar if b == 0 and part % 2 == 1 else on_vector)
-                load_behind((b, kind, part))
-            if live(step - 4):
+            for b, part, engine, first, last in V_PLAN.get(step, []):
+                group_v((b, V_KIND, part), {"S": on_scalar, "V": on_vector, "G": on_gpsimd}[engine], first, last)
+                if last == BANK:
+                    load_behind((b, V_KIND, part))
+            if step >= 4:
                 copy_context(step - 4, 0, on_scalar)
             if live(step):
                 exponentials(step)
-            for unit in v_units:
-                quantise_unit(unit)
-            if live(step - 1):
+            for b, part in V_QUANT.get(step, []):
+                quantise_unit((b, V_KIND, part))
+            if live(step - 1) and step < TILES - 1:
                 invert_sum(step - 1)
-                normalise(step - 1)
-            if live(step - 4):
-                copy_context(step - 4, 1, on_scalar if v_units else on_vector)
+                normalise(step - 1, nc.gpsimd.tensor_scalar)
+            if step >= 4:
+                copy_context(step - 4, 1, on_vector if step in CTX_V else on_scalar)
+
+        last = TILES - 1
+        context_matmuls(last - 3)
+        transpose_attn(last - 1, "scores")
+        group_attn(last - 2, on_both)
+        quantise_attn(last - 2)
+        invert_sum(last)
+        normalise(last, nc.vector.tensor_scalar)
+        context_matmuls(last - 2, "flipped")
+        transpose_attn(last)
+        group_attn(last - 1, on_both)
+        quantise_attn(last - 1)
+        copy_context(last - 3, 0, on_scalar)
+        copy_context(last - 3, 1, on_vector)
+        group_attn(last, on_both)
+        quantise_attn(last)
+        context_matmuls(last - 1)
+        copy_context(last - 2, 0, on_scalar)
+        copy_context(last - 2, 1, on_vector)
+        context_matmuls(last, "scores")
+        for half in range(2):
+            copy_context(last - 1, half, on_both[half])
+        for half in range(2):
+            copy_context(last, half, on_both[half])

@@ -36,13 +36,13 @@ ROW_UNITS = [(b, kind, part) for b in range(BATCH) for kind, part in ROW_ORDER]
 V_UNITS = [(b, V_KIND, part) for b in range(BATCH) for part in range(PARTS)]
 ROW_HEAD = 1 + PARTS
 V_STEP = 6
-V_PLAN = {0: [(0, 0, "V", 0, 512)], 1: [(0, 1, "S", 0, 512)], 2: [(0, 2, "V", 0, 512)], 3: [(0, 3, "S", 0, 512)], 6: [(1, 0, "S", 0, 64), (1, 0, "V", 64, 512)], 7: [(1, 1, "S", 0, 64), (1, 1, "V", 64, 512)], 8: [(1, 2, "S", 0, 64), (1, 2, "V", 64, 512)], 9: [(1, 3, "S", 0, 64), (1, 3, "V", 64, 512)]}
+V_PLAN = {0: [(0, 0, "S", 0, 128), (0, 0, "V", 128, 512)], 1: [(0, 1, "S", 0, 384), (0, 1, "V", 384, 512)], 2: [(0, 2, "S", 0, 128), (0, 2, "V", 128, 512)], 3: [(0, 3, "S", 0, 512)], 6: [(1, 0, "S", 0, 64), (1, 0, "V", 64, 512)], 7: [(1, 1, "S", 0, 64), (1, 1, "V", 64, 512)], 8: [(1, 2, "S", 0, 64), (1, 2, "V", 64, 512)], 9: [(1, 3, "S", 0, 64), (1, 3, "V", 64, 512)]}
 V_QUANT = {3: [(0, 3)]}
 V_LATE = {1: [(0, 0)], 2: [(0, 1)], 3: [(0, 2)], 7: [(1, 0)], 8: [(1, 1)], 9: [(1, 2)], 10: [(1, 3)]}
 V_LOADS = {0: [(0, 0)], 1: [(0, 1)], 2: [(0, 2)], 3: [(0, 3)], 6: [(1, 0)], 7: [(1, 1)], 8: [(1, 2)], 9: [(1, 3)]}
 ROW_STEPS = {n: [5 + n] for n in range(11)}
 CTX_V = (4, 5, 10, 11, 12, 13, 14, 15)
-RAW_RING = 15
+RAW_RING = 14
 OUT_TILES = 2
 PSUM_TAGS = ("flipped", "scores", "attn_t", "context")
 
@@ -61,7 +61,7 @@ def tile_multiheadattention_tupe_pb_kernel(tc, q, k, v, pos_bias, out, attn):
         psum = ctx.enter_context(tc.psum_pool(name="psum", bufs=2))
         ctx.enter_context(tc.manual_schedule())
 
-        raw, grouped, codes, scales = {}, {}, {}, {}
+        raw, grouped, codes, scales, k_codes, k_scales = {}, {}, {}, {}, {}, {}
         bias = {}
 
         def load_unit(unit, tiles=slice(0, 2)):
@@ -143,7 +143,24 @@ def tile_multiheadattention_tupe_pb_kernel(tc, q, k, v, pos_bias, out, attn):
                 in_=raw[unit][:].rearrange("p (j c i) -> p c j i", j=PACK, i=4)[:, first // 4 : last // 4],
             )
 
+        def quantise_k(unit):
+            b, kind, part = unit
+            half, side = divmod(part, 2)
+            if (b, half) not in k_codes:
+                k_codes[b, half] = operands.tile([P, PASSES, BANK], U32, name="k_codes%d%d" % (b, half), align_bytes=64)
+                k_scales[b, half] = operands.tile([P, PASSES, BANK], U8, name="k_scales%d%d" % (b, half), align_bytes=64)
+            mine = slice(UNIT_ROWS * side, UNIT_ROWS * (side + 1))
+            for g in range(PASSES):
+                nc.vector.quantize_mx(
+                    out=k_codes[b, half][:, g, mine].bitcast(FP8X4),
+                    scales=k_scales[b, half][:, g, mine],
+                    in_=grouped[unit][:, LENGTH * g : LENGTH * (g + 1)],
+                )
+
         def quantise_unit(unit, first=0, last=UNIT_WORDS):
+            if unit[1] == K_KIND:
+                quantise_k(unit)
+                return
             if unit not in codes:
                 codes[unit] = operands.tile([P, UNIT_WORDS], U32, name="codes%d%d%d" % unit, align_bytes=64)
                 scales[unit] = operands.tile([P, UNIT_WORDS], U8, name="scales%d%d%d" % unit, align_bytes=64)
@@ -164,21 +181,18 @@ def tile_multiheadattention_tupe_pb_kernel(tc, q, k, v, pos_bias, out, attn):
             for half in range(2):
                 bank = psum.tile([P, BANK], F32, name="scores")
                 score_banks[i].append(bank)
-                for part in (2 * half, 2 * half + 1):
-                    keys_unit = (b, K_KIND, part)
-                    for g in range(PASSES):
-                        first = UNIT_ROWS * (m % 2) + P * g
-                        mine = slice(first, first + P)
-                        keys = slice(UNIT_ROWS * g, UNIT_ROWS * (g + 1))
-                        nc.tensor.matmul_mx(
-                            out=bank[:, UNIT_ROWS * (part % 2) : UNIT_ROWS * (part % 2 + 1)],
-                            lhsT=codes[mine_unit][:, mine].bitcast(FP8X4),
-                            lhsT_scale=scales[mine_unit][:, mine],
-                            rhs=codes[keys_unit][:, keys].bitcast(FP8X4),
-                            rhs_scale=scales[keys_unit][:, keys],
-                            start=(g == 0),
-                            stop=(g == PASSES - 1),
-                        )
+                for g in range(PASSES):
+                    first = UNIT_ROWS * (m % 2) + P * g
+                    mine = slice(first, first + P)
+                    nc.tensor.matmul_mx(
+                        out=bank[:],
+                        lhsT=codes[mine_unit][:, mine].bitcast(FP8X4),
+                        lhsT_scale=scales[mine_unit][:, mine],
+                        rhs=k_codes[b, half][:, g].bitcast(FP8X4),
+                        rhs_scale=k_scales[b, half][:, g],
+                        start=(g == 0),
+                        stop=(g == PASSES - 1),
+                    )
 
         def add_bias(i):
             m = i % TILES_PER_BATCH
@@ -234,51 +248,44 @@ def tile_multiheadattention_tupe_pb_kernel(tc, q, k, v, pos_bias, out, attn):
                 copies[g](out=attn_grouped[i][:, g], in_=attn_t[i][g][:].rearrange("p j s -> p s j"))
 
         def quantise_attn(i):
-            attn_codes[i] = stage.tile([P, PASSES * P], U32, name="attn_codes", align_bytes=64)
-            attn_scales[i] = stage.tile([P, PASSES * P], U8, name="attn_scales", align_bytes=64)
-            nc.vector.quantize_mx(
-                out=attn_codes[i][:].bitcast(FP8X4),
-                scales=attn_scales[i][:],
-                in_=attn_grouped[i][:].rearrange("p g s j -> p (g s j)"),
-            )
+            pair, t = divmod(i, 2)
+            if t == 0:
+                attn_codes[pair] = stage.tile([P, PASSES, UNIT_ROWS], U32, name="attn_codes", align_bytes=64, bufs=3)
+                attn_scales[pair] = stage.tile([P, PASSES, UNIT_ROWS], U8, name="attn_scales", align_bytes=64, bufs=3)
+            mine = slice(P * t, P * (t + 1))
+            for g in range(PASSES):
+                nc.vector.quantize_mx(
+                    out=attn_codes[pair][:, g, mine].bitcast(FP8X4),
+                    scales=attn_scales[pair][:, g, mine],
+                    in_=attn_grouped[i][:, g].rearrange("p s j -> p (s j)"),
+                )
 
-        def context_matmuls(i, banks="context"):
-            b = i // TILES_PER_BATCH
-            context_banks[i] = []
-            for half in range(2):
-                bank = psum.tile([P, 4, P], F32, name="context", tag=banks)
-                context_banks[i].append(bank)
-                for f in range(4):
+        def context_matmuls(pair, half, banks="context"):
+            b = pair // (TILES_PER_BATCH // 2)
+            for c in range(2):
+                bank = psum.tile([P, 2, UNIT_ROWS], F32, name="context", tag=banks)
+                context_banks[pair, half, c] = bank
+                for f in (2 * c, 2 * c + 1):
                     for g in range(PASSES):
                         v_unit = (b, V_KIND, PASSES * half + g)
                         feats = slice(P * f, P * (f + 1))
-                        mine = slice(P * g, P * (g + 1))
                         nc.tensor.matmul_mx(
-                            out=bank[:, f, :],
+                            out=bank[:, f % 2, :],
                             lhsT=codes[v_unit][:, feats].bitcast(FP8X4),
                             lhsT_scale=scales[v_unit][:, feats],
-                            rhs=attn_codes[i][:, mine].bitcast(FP8X4),
-                            rhs_scale=attn_scales[i][:, mine],
+                            rhs=attn_codes[pair][:, g].bitcast(FP8X4),
+                            rhs_scale=attn_scales[pair][:, g],
                             start=(g == 0),
                             stop=(g == PASSES - 1),
                         )
 
-        def copy_context(i, half, copy):
-            b, m = divmod(i, TILES_PER_BATCH)
-            rows = out[b, BANK * half : BANK * (half + 1), :].rearrange("(f p) s -> p f s", p=P)
-            if i >= TILES - 4:
-                if half == 0:
-                    out_sb[i] = raw_pool.tile([P, UNIT_COLS], BF16, name="raw")
-                mine = out_sb[i][:, LENGTH * half : LENGTH * (half + 1)].bitcast(F32).rearrange("p (f s) -> p f s", f=4)
-                copy(out=mine, in_=context_banks[i][half][:])
-                nc.sync.dma_start(out=rows[:, :, P * m : P * (m + 1)], in_=mine)
-                return
-            first, place = i - i % OUT_TILES, i % OUT_TILES
-            if place == 0:
-                out_sb[first, half] = out_pool.tile([P, 4, OUT_TILES * P], F32, name="out_sb")
-            copy(out=out_sb[first, half][:, :, P * place : P * (place + 1)], in_=context_banks[i][half][:])
-            if place == OUT_TILES - 1:
-                nc.sync.dma_start(out=rows[:, :, P * (m - place) : P * (m + 1)], in_=out_sb[first, half][:])
+        def copy_context(pair, half, c, copy):
+            b, first = divmod(2 * P * pair, LENGTH)
+            if c == 0:
+                out_sb[pair, half] = out_pool.tile([P, 4, UNIT_ROWS], F32, name="out_sb", bufs=4)
+            copy(out=out_sb[pair, half][:, 2 * c : 2 * c + 2, :], in_=context_banks[pair, half, c][:])
+            rows = out[b, BANK * half : BANK * (half + 1), first : first + UNIT_ROWS].rearrange("(f p) s -> p f s", p=P)
+            nc.sync.dma_start(out=rows[:, 2 * c : 2 * c + 2, :], in_=out_sb[pair, half][:, 2 * c : 2 * c + 2, :])
 
         on_scalar, on_vector = nc.scalar.copy, nc.vector.tensor_copy
 
@@ -334,8 +341,9 @@ def tile_multiheadattention_tupe_pb_kernel(tc, q, k, v, pos_bias, out, attn):
             row_units, v_units = units_of_step(step)
             for unit in row_units:
                 prepare_rows(unit, "flipped", (on_scalar, on_scalar))
-            if step >= 4:
-                context_matmuls(step - 4)
+            if step >= 5:
+                halves_done = divmod(step - 5, 2)
+                context_matmuls(*halves_done)
             if step >= 3:
                 group_attn(step - 3, (on_scalar, on_scalar))
             if live(step):
@@ -364,8 +372,8 @@ def tile_multiheadattention_tupe_pb_kernel(tc, q, k, v, pos_bias, out, attn):
                 group_v((b, V_KIND, part), {"S": on_scalar, "V": on_vector, "G": on_gpsimd}[engine], first, last)
                 if last == BANK:
                     load_behind((b, V_KIND, part))
-            if step >= 4:
-                copy_context(step - 4, 0, on_scalar)
+            if step >= 5:
+                copy_context(*halves_done, 0, on_scalar)
             if live(step):
                 exponentials(step)
             for b, part in V_QUANT.get(step, []):
@@ -373,29 +381,32 @@ def tile_multiheadattention_tupe_pb_kernel(tc, q, k, v, pos_bias, out, attn):
             if live(step - 1) and step < TILES - 1:
                 invert_sum(step - 1)
                 normalise(step - 1, nc.gpsimd.tensor_scalar)
-            if step >= 4:
-                copy_context(step - 4, 1, on_vector if step in CTX_V else on_scalar)
+            if step >= 5:
+                copy_context(*halves_done, 1, on_vector if step in CTX_V else on_scalar)
 
         last = TILES - 1
-        context_matmuls(last - 3)
+        end = last // 2
+        context_matmuls(end - 2, 1)
         transpose_attn(last - 1, "scores")
         group_attn(last - 2, on_both)
         quantise_attn(last - 2)
         invert_sum(last)
         normalise(last, nc.vector.tensor_scalar)
-        context_matmuls(last - 2, "flipped")
+        context_matmuls(end - 1, 0, "flipped")
         transpose_attn(last)
         group_attn(last - 1, on_both)
         quantise_attn(last - 1)
-        copy_context(last - 3, 0, on_scalar)
-        copy_context(last - 3, 1, on_vector)
+        for c in range(2):
+            copy_context(end - 2, 1, c, on_both[c])
         group_attn(last, on_both)
         quantise_attn(last)
-        context_matmuls(last - 1)
-        copy_context(last - 2, 0, on_scalar)
-        copy_context(last - 2, 1, on_vector)
-        context_matmuls(last, "scores")
+        context_matmuls(end - 1, 1)
+        for c in range(2):
+            copy_context(end - 1, 0, c, on_both[c])
+        context_matmuls(end, 0, "scores")
+        for c in range(2):
+            copy_context(end - 1, 1, c, on_both[c])
+        context_matmuls(end, 1, "flipped")
         for half in range(2):
-            copy_context(last - 1, half, on_both[half])
-        for half in range(2):
-            copy_context(last, half, on_both[half])
+            for c in range(2):
+                copy_context(end, half, c, on_both[c])

@@ -36,7 +36,7 @@ ROW_UNITS = [(b, kind, part) for b in range(BATCH) for kind, part in ROW_ORDER]
 V_UNITS = [(b, V_KIND, part) for b in range(BATCH) for part in range(PARTS)]
 ROW_HEAD = 1 + PARTS
 V_STEP = 6
-V_PLAN = {0: [(0, 0, "S", 0, 128), (0, 0, "V", 128, 512)], 1: [(0, 1, "S", 0, 384), (0, 1, "V", 384, 512)], 2: [(0, 2, "S", 0, 128), (0, 2, "V", 128, 512)], 3: [(0, 3, "S", 0, 512)], 6: [(1, 0, "S", 0, 64), (1, 0, "V", 64, 512)], 7: [(1, 1, "S", 0, 64), (1, 1, "V", 64, 512)], 8: [(1, 2, "S", 0, 64), (1, 2, "V", 64, 512)], 9: [(1, 3, "S", 0, 64), (1, 3, "V", 64, 512)]}
+V_PLAN = {0: [(0, 0, "S", 0, 256), (0, 0, "V", 256, 512)], 1: [(0, 1, "S", 0, 384), (0, 1, "V", 384, 512)], 2: [(0, 2, "S", 0, 128), (0, 2, "V", 128, 512)], 3: [(0, 3, "S", 0, 512)], 6: [(1, 0, "G", 0, 128), (1, 0, "V", 128, 512)], 7: [(1, 1, "G", 0, 128), (1, 1, "V", 128, 512)], 8: [(1, 2, "G", 0, 128), (1, 2, "V", 128, 512)], 9: [(1, 3, "G", 0, 128), (1, 3, "V", 128, 512)]}
 V_QUANT = {3: [(0, 3)]}
 V_LATE = {1: [(0, 0)], 2: [(0, 1)], 3: [(0, 2)], 7: [(1, 0)], 8: [(1, 1)], 9: [(1, 2)], 10: [(1, 3)]}
 V_LOADS = {0: [(0, 0)], 1: [(0, 1)], 2: [(0, 2)], 3: [(0, 3)], 6: [(1, 0)], 7: [(1, 1)], 8: [(1, 2)], 9: [(1, 3)]}

@@ -78,10 +78,13 @@ def tile_multiheadattention_tupe_pb_kernel(tc, q, k, v, pos_bias, out, attn):
             else:
                 x = k if kind == K_KIND else q
                 rows = x[b, UNIT_ROWS * part : UNIT_ROWS * (part + 1), :]
-                nc.sync.dma_start(
-                    out=raw[unit][:].rearrange("p (t d) -> p t d", t=2)[:, tiles],
-                    in_=rows.rearrange("(t p) d -> p t d", p=P)[:, tiles],
-                )
+                if kind == K_KIND:
+                    nc.sync.dma_start(out=raw[unit][:], in_=rows.rearrange("(p t) d -> p (t d)", t=2))
+                else:
+                    nc.sync.dma_start(
+                        out=raw[unit][:].rearrange("p (t d) -> p t d", t=2)[:, tiles],
+                        in_=rows.rearrange("(t p) d -> p t d", p=P)[:, tiles],
+                    )
 
         def load_bias(pair):
             bias[pair] = const.tile([P, 2, LENGTH], BF16, name="bias%d" % pair)
@@ -105,8 +108,8 @@ def tile_multiheadattention_tupe_pb_kernel(tc, q, k, v, pos_bias, out, attn):
             grouped_words = grouped[unit][:].bitcast(F32)
             for g in range(PASSES):
                 copies[g](
-                    out=grouped_words[:, BANK * g : BANK * (g + 1)].rearrange("p (r h) -> p r h", h=2),
-                    in_=flipped[g][:].rearrange("p h r -> p r h"),
+                    out=grouped_words[:, BANK * g : BANK * (g + 1)].rearrange("p (r t h) -> p r t h", t=2, h=2),
+                    in_=flipped[g][:].rearrange("p h (t r) -> p r t h", t=2),
                 )
 
         def flip_q(unit, t, banks):

@@ -78,18 +78,15 @@ def tile_multiheadattention_tupe_pb_kernel(tc, q, k, v, pos_bias, out, attn):
             else:
                 x = k if kind == K_KIND else q
                 rows = x[b, UNIT_ROWS * part : UNIT_ROWS * (part + 1), :]
-                if kind == K_KIND:
-                    nc.sync.dma_start(out=raw[unit][:], in_=rows.rearrange("(p t) d -> p (t d)", t=2))
-                else:
-                    nc.sync.dma_start(
-                        out=raw[unit][:].rearrange("p (t d) -> p t d", t=2)[:, tiles],
-                        in_=rows.rearrange("(t p) d -> p t d", p=P)[:, tiles],
-                    )
+                nc.sync.dma_start(
+                    out=raw[unit][:].rearrange("p (t d) -> p t d", t=2)[:, tiles],
+                    in_=rows.rearrange("(p t) d -> p t d", t=2)[:, tiles],
+                )
 
         def load_bias(pair):
             bias[pair] = const.tile([P, 2, LENGTH], BF16, name="bias%d" % pair)
             rows = pos_bias[2 * P * pair : 2 * P * (pair + 1), :]
-            nc.sync.dma_start(out=bias[pair][:], in_=rows.rearrange("(t p) c -> p t c", p=P))
+            nc.sync.dma_start(out=bias[pair][:], in_=rows.rearrange("(p t) c -> p t c", t=2))
 
         def flip_k(unit, banks):
             words = raw[unit][:].bitcast(F32)
@@ -234,7 +231,8 @@ def tile_multiheadattention_tupe_pb_kernel(tc, q, k, v, pos_bias, out, attn):
             b, m = divmod(i, TILES_PER_BATCH)
             attn_sb[i] = attn_pool.tile([P, LENGTH], F32, name="attn_sb")
             multiply(out=attn_sb[i][:], in0=expd[i][:], scalar1=inv_sum[i][:], scalar2=0.0, op0=MULT, op1=ADD)
-            nc.sync.dma_start(out=attn[b, P * m : P * (m + 1), :], in_=attn_sb[i][:])
+            rows = attn[b, UNIT_ROWS * (m // 2) : UNIT_ROWS * (m // 2 + 1), :].rearrange("(p t) c -> p t c", t=2)
+            nc.sync.dma_start(out=rows[:, m % 2], in_=attn_sb[i][:])
 
         def transpose_attn(i, banks="attn_t"):
             attn_t[i] = []
@@ -286,7 +284,10 @@ def tile_multiheadattention_tupe_pb_kernel(tc, q, k, v, pos_bias, out, attn):
             b, first = divmod(2 * P * pair, LENGTH)
             if c == 0:
                 out_sb[pair, half] = out_pool.tile([P, 4, UNIT_ROWS], F32, name="out_sb", bufs=4)
-            copy(out=out_sb[pair, half][:, 2 * c : 2 * c + 2, :], in_=context_banks[pair, half, c][:])
+            copy(
+                out=out_sb[pair, half][:, 2 * c : 2 * c + 2, :].rearrange("p f (s t) -> p f s t", t=2),
+                in_=context_banks[pair, half, c][:].rearrange("p f (t s) -> p f s t", t=2),
+            )
             rows = out[b, BANK * half : BANK * (half + 1), first : first + UNIT_ROWS].rearrange("(f p) s -> p f s", p=P)
             nc.sync.dma_start(out=rows[:, 2 * c : 2 * c + 2, :], in_=out_sb[pair, half][:, 2 * c : 2 * c + 2, :])
 

import math
from contextlib import ExitStack

import concourse.mybir as mybir
from concourse.masks import make_identity

F32 = mybir.dt.float32
BF16 = mybir.dt.bfloat16
U32 = mybir.dt.uint32
U8 = mybir.dt.uint8
FP8X4 = mybir.dt.float8_e4m3fn_x4
ADD = mybir.AluOpType.add
MULT = mybir.AluOpType.mult
MAX = mybir.AluOpType.max
EXP = mybir.ActivationFunctionType.Exp
ALONG_ROW = mybir.AxisListType.X

P = 128
PACK = 4
K_PASS = P * PACK
BATCH, LENGTH = 2, 1024
PASSES = LENGTH // K_PASS
BANK = 512
INV_SCALE = 1.0 / math.sqrt(2.0 * 64)
FLOPS = 2 * 2 * BATCH * LENGTH * LENGTH * LENGTH

TILES_PER_BATCH = LENGTH // P
TILES = BATCH * TILES_PER_BATCH
UNIT_COLS = 2048
UNIT_WORDS = UNIT_COLS // PACK
UNIT_ROWS = 256
K_KIND, Q_KIND, V_KIND = 0, 1, 2
PARTS = 4
ROW_ORDER = [(Q_KIND, 0)] + [(K_KIND, part) for part in range(PARTS)] + [(Q_KIND, part) for part in range(1, PARTS)]
ROW_UNITS = [(b, kind, part) for b in range(BATCH) for kind, part in ROW_ORDER]
V_UNITS = [(b, V_KIND, part) for b in range(BATCH) for part in range(PARTS)]
ROW_HEAD = 1 + PARTS
V_STEP = 6
V_PLAN = {0: [(0, 0, "S", 0, 256), (0, 0, "V", 256, 512)], 1: [(0, 1, "S", 0, 384), (0, 1, "V", 384, 512)], 2: [(0, 2, "S", 0, 128), (0, 2, "V", 128, 512)], 3: [(0, 3, "S", 0, 512)], 6: [(1, 0, "G", 0, 128), (1, 0, "V", 128, 512)], 7: [(1, 1, "G", 0, 128), (1, 1, "V", 128, 512)], 8: [(1, 2, "G", 0, 128), (1, 2, "V", 128, 512)], 9: [(1, 3, "G", 0, 128), (1, 3, "V", 128, 512)]}
V_QUANT = {3: [(0, 3)]}
V_LATE = {1: [(0, 0)], 2: [(0, 1)], 3: [(0, 2)], 7: [(1, 0)], 8: [(1, 1)], 9: [(1, 2)], 10: [(1, 3)]}
V_LOADS = {0: [(0, 0)], 1: [(0, 1)], 2: [(0, 2)], 3: [(0, 3)], 6: [(1, 0)], 7: [(1, 1)], 8: [(1, 2)], 9: [(1, 3)]}
ROW_STEPS = {n: [5 + n] for n in range(11)}
CTX_V = (4, 5, 10, 11, 12, 13, 14, 15)
RAW_RING = 14
OUT_TILES = 2
PSUM_TAGS = ("flipped", "scores", "attn_t", "context")


def tile_multiheadattention_tupe_pb_kernel(tc, q, k, v, pos_bias, out, attn):
    nc = tc.nc
    with ExitStack() as ctx:
        const = ctx.enter_context(tc.tile_pool(name="const", bufs=1))
        raw_pool = ctx.enter_context(tc.tile_pool(name="raw", bufs=RAW_RING))
        operands = ctx.enter_context(tc.tile_pool(name="operands", bufs=1))
        stage = ctx.enter_context(tc.tile_pool(name="stage", bufs=4))
        soft = ctx.enter_context(tc.tile_pool(name="soft", bufs=2))
        attn_pool = ctx.enter_context(tc.tile_pool(name="attn", bufs=5))
        stats = ctx.enter_context(tc.tile_pool(name="stats", bufs=3))
        out_pool = ctx.enter_context(tc.tile_pool(name="out", bufs=4))
        psum = ctx.enter_context(tc.psum_pool(name="psum", bufs=2))
        ctx.enter_context(tc.manual_schedule())

        raw, grouped, codes, scales, k_codes, k_scales = {}, {}, {}, {}, {}, {}
        bias = {}

        def load_unit(unit, tiles=slice(0, 2)):
            b, kind, part = unit
            if unit not in raw:
                raw[unit] = raw_pool.tile([P, UNIT_COLS], BF16, name="raw")
            if kind == V_KIND:
                half, g = divmod(part, PASSES)
                rows = v[b, K_PASS * g : K_PASS * (g + 1), BANK * half : BANK * (half + 1)]
                nc.sync.dma_start(
                    out=raw[unit][:].rearrange("p (j d) -> p j d", j=PACK),
                    in_=rows.rearrange("(j p) d -> p j d", p=P),
                )
            else:
                x = k if kind == K_KIND else q
                rows = x[b, UNIT_ROWS * part : UNIT_ROWS * (part + 1), :]
                nc.sync.dma_start(
                    out=raw[unit][:].rearrange("p (t d) -> p t d", t=2)[:, tiles],
                    in_=rows.rearrange("(p t) d -> p t d", t=2)[:, tiles],
                )

        def load_bias(pair):
            bias[pair] = const.tile([P, 2, LENGTH], BF16, name="bias%d" % pair)
            rows = pos_bias[2 * P * pair : 2 * P * (pair + 1), :]
            nc.sync.dma_start(out=bias[pair][:], in_=rows.rearrange("(p t) c -> p t c", t=2))

        def flip_k(unit, banks):
            words = raw[unit][:].bitcast(F32)
            flipped = [psum.tile([P, 2, UNIT_ROWS], F32, name="flipped", tag=banks) for g in range(PASSES)]
            for g in range(PASSES):
                for t in range(2):
                    for h in range(2):
                        first = BANK * t + 256 * g + P * h
                        nc.tensor.transpose(
                            flipped[g][:, h, P * t : P * (t + 1)], words[:, first : first + P], ident[:]
                        )
            return flipped

        def group_k(unit, flipped, copies):
            grouped[unit] = stage.tile([P, UNIT_COLS], BF16, name="grouped", align_bytes=64)
            grouped_words = grouped[unit][:].bitcast(F32)
            for g in range(PASSES):
                copies[g](
                    out=grouped_words[:, BANK * g : BANK * (g + 1)].rearrange("p (r t h) -> p r t h", t=2, h=2),
                    in_=flipped[g][:].rearrange("p h (t r) -> p r t h", t=2),
                )

        def flip_q(unit, t, banks):
            words = raw[unit][:].bitcast(F32)
            flipped = psum.tile([P, PASSES, 2, P], F32, name="flipped", tag=banks)
            for g in range(PASSES):
                for h in range(2):
                    first = BANK * t + 256 * g + P * h
                    nc.tensor.transpose(flipped[:, g, h, :], words[:, first : first + P], ident[:])
            return flipped

        def group_q(unit, t, flipped, copy):
            if unit not in grouped:
                grouped[unit] = stage.tile([P, UNIT_COLS], BF16, name="grouped", align_bytes=64)
            copy(
                out=grouped[unit][:].bitcast(F32)[:, BANK * t : BANK * (t + 1)].rearrange("p (g r h) -> p g r h", g=PASSES, h=2),
                in_=flipped[:].rearrange("p g h r -> p g r h"),
            )

        def prepare_rows(unit, banks, copies):
            if unit[1] == K_KIND:
                group_k(unit, flip_k(unit, banks), copies)
            else:
                both = [flip_q(unit, t, banks) for t in range(2)]
                for t in range(2):
                    group_q(unit, t, both[t], copies[t])
            load_behind(unit)

        def group_v(unit, copy, first, last):
            if unit not in grouped:
                grouped[unit] = stage.tile([P, UNIT_COLS], BF16, name="grouped_v", align_bytes=64, bufs=4)
            copy(
                out=grouped[unit][:, PACK * first : PACK * last].rearrange("p (c i j) -> p c j i", i=4, j=PACK),
                in_=raw[unit][:].rearrange("p (j c i) -> p c j i", j=PACK, i=4)[:, first // 4 : last // 4],
            )

        def quantise_k(unit):
            b, kind, part = unit
            half, side = divmod(part, 2)
            if (b, half) not in k_codes:
                k_codes[b, half] = operands.tile([P, PASSES, BANK], U32, name="k_codes%d%d" % (b, half), align_bytes=64)
                k_scales[b, half] = operands.tile([P, PASSES, BANK], U8, name="k_scales%d%d" % (b, half), align_bytes=64)
            mine = slice(UNIT_ROWS * side, UNIT_ROWS * (side + 1))
            for g in range(PASSES):
                nc.vector.quantize_mx(
                    out=k_codes[b, half][:, g, mine].bitcast(FP8X4),
                    scales=k_scales[b, half][:, g, mine],
                    in_=grouped[unit][:, LENGTH * g : LENGTH * (g + 1)],
                )

        def quantise_unit(unit, first=0, last=UNIT_WORDS):
            if unit[1] == K_KIND:
                quantise_k(unit)
                return
            if unit not in codes:
                codes[unit] = operands.tile([P, UNIT_WORDS], U32, name="codes%d%d%d" % unit, align_bytes=64)
                scales[unit] = operands.tile([P, UNIT_WORDS], U8, name="scales%d%d%d" % unit, align_bytes=64)
            nc.vector.quantize_mx(
                out=codes[unit][:, first:last].bitcast(FP8X4),
                scales=scales[unit][:, first:last],
                in_=grouped[unit][:, PACK * first : PACK * last],
            )

        score_banks, summed, half_max, shift, row_sum, inv_sum = {}, {}, {}, {}, {}, {}
        expd, attn_sb, attn_t, attn_grouped, attn_codes, attn_scales = {}, {}, {}, {}, {}, {}
        context_banks, out_sb = {}, {}

        def score_matmuls(i):
            b, m = divmod(i, TILES_PER_BATCH)
            mine_unit = (b, Q_KIND, m // 2)
            score_banks[i] = []
            for half in range(2):
                bank = psum.tile([P, BANK], F32, name="scores")
                score_banks[i].append(bank)
                for g in range(PASSES):
                    first = UNIT_ROWS * (m % 2) + P * g
                    mine = slice(first, first + P)
                    nc.tensor.matmul_mx(
                        out=bank[:],
                        lhsT=codes[mine_unit][:, mine].bitcast(FP8X4),
                        lhsT_scale=scales[mine_unit][:, mine],
                        rhs=k_codes[b, half][:, g].bitcast(FP8X4),
                        rhs_scale=k_scales[b, half][:, g],
                        start=(g == 0),
                        stop=(g == PASSES - 1),
                    )

        def add_bias(i):
            m = i % TILES_PER_BATCH
            summed[i] = soft.tile([P, LENGTH], F32, name="summed")
            for half in range(2):
                cols = slice(BANK * half, BANK * (half + 1))
                nc.vector.tensor_tensor(
                    out=summed[i][:, cols], in0=score_banks[i][half][:], in1=bias[m // 2][:, m % 2, cols], op=ADD
                )

        def find_maxima(i):
            half_max[i] = []
            for half in range(2):
                cols = slice(BANK * half, BANK * (half + 1))
                half_max[i].append(stats.tile([P, 1], F32, name="half_max%d" % half))
                nc.vector.tensor_reduce(out=half_max[i][half][:], in_=summed[i][:, cols], axis=ALONG_ROW, op=MAX)

        def find_shift(i):
            shift[i] = stats.tile([P, 1], F32, name="shift")
            nc.vector.tensor_scalar(
                out=shift[i][:], in0=half_max[i][0][:], scalar1=half_max[i][1][:], scalar2=-INV_SCALE, op0=MAX, op1=MULT
            )

        def exponentials(i):
            expd[i] = soft.tile([P, LENGTH], F32, name="expd", bufs=3)
            row_sum[i] = stats.tile([P, 1], F32, name="row_sum")
            nc.scalar.activation(
                out=expd[i][:], in_=summed[i][:], func=EXP, bias=shift[i][:], scale=INV_SCALE, accum_out=row_sum[i][:]
            )

        def invert_sum(i):
            inv_sum[i] = stats.tile([P, 1], F32, name="inv_sum")
            nc.vector.reciprocal(out=inv_sum[i][:], in_=row_sum[i][:])

        def normalise(i, multiply):
            b, m = divmod(i, TILES_PER_BATCH)
            attn_sb[i] = attn_pool.tile([P, LENGTH], F32, name="attn_sb")
            multiply(out=attn_sb[i][:], in0=expd[i][:], scalar1=inv_sum[i][:], scalar2=0.0, op0=MULT, op1=ADD)
            rows = attn[b, UNIT_ROWS * (m // 2) : UNIT_ROWS * (m // 2 + 1), :].rearrange("(p t) c -> p t c", t=2)
            nc.sync.dma_start(out=rows[:, m % 2], in_=attn_sb[i][:])

        def transpose_attn(i, banks="attn_t"):
            attn_t[i] = []
            for g in range(PASSES):
                bank = psum.tile([P, PACK, P], F32, name="attn_t", tag=banks)
                attn_t[i].append(bank)
                for j in range(PACK):
                    first = K_PASS * g + P * j
                    nc.tensor.transpose(bank[:, j, :], attn_sb[i][:, first : first + P], ident[:])

        def group_attn(i, copies):
            attn_grouped[i] = stage.tile([P, PASSES, P, PACK], BF16, name="attn_grouped", align_bytes=64)
            for g in range(PASSES):
                copies[g](out=attn_grouped[i][:, g], in_=attn_t[i][g][:].rearrange("p j s -> p s j"))

        def quantise_attn(i):
            pair, t = divmod(i, 2)
            if t == 0:
                attn_codes[pair] = stage.tile([P, PASSES, UNIT_ROWS], U32, name="attn_codes", align_bytes=64, bufs=3)
                attn_scales[pair] = stage.tile([P, PASSES, UNIT_ROWS], U8, name="attn_scales", align_bytes=64, bufs=3)
            mine = slice(P * t, P * (t + 1))
            for g in range(PASSES):
                nc.vector.quantize_mx(
                    out=attn_codes[pair][:, g, mine].bitcast(FP8X4),
                    scales=attn_scales[pair][:, g, mine],
                    in_=attn_grouped[i][:, g].rearrange("p s j -> p (s j)"),
                )

        def context_matmuls(pair, half, banks="context"):
            b = pair // (TILES_PER_BATCH // 2)
            for c in range(2):
                bank = psum.tile([P, 2, UNIT_ROWS], F32, name="context", tag=banks)
                context_banks[pair, half, c] = bank
                for f in (2 * c, 2 * c + 1):
                    for g in range(PASSES):
                        v_unit = (b, V_KIND, PASSES * half + g)
                        feats = slice(P * f, P * (f + 1))
                        nc.tensor.matmul_mx(
                            out=bank[:, f % 2, :],
                            lhsT=codes[v_unit][:, feats].bitcast(FP8X4),
                            lhsT_scale=scales[v_unit][:, feats],
                            rhs=attn_codes[pair][:, g].bitcast(FP8X4),
                            rhs_scale=attn_scales[pair][:, g],
                            start=(g == 0),
                            stop=(g == PASSES - 1),
                        )

        def copy_context(pair, half, c, copy):
            b, first = divmod(2 * P * pair, LENGTH)
            if c == 0:
                out_sb[pair, half] = out_pool.tile([P, 4, UNIT_ROWS], F32, name="out_sb", bufs=4)
            copy(
                out=out_sb[pair, half][:, 2 * c : 2 * c + 2, :].rearrange("p f (s t) -> p f s t", t=2),
                in_=context_banks[pair, half, c][:].rearrange("p f (t s) -> p f s t", t=2),
            )
            rows = out[b, BANK * half : BANK * (half + 1), first : first + UNIT_ROWS].rearrange("(f p) s -> p f s", p=P)
            nc.sync.dma_start(out=rows[:, 2 * c : 2 * c + 2, :], in_=out_sb[pair, half][:, 2 * c : 2 * c + 2, :])

        on_scalar, on_vector = nc.scalar.copy, nc.vector.tensor_copy

        def on_gpsimd(out, in_):
            nc.gpsimd.tensor_scalar(out=out, in0=in_, scalar1=1.0, scalar2=0.0, op0=MULT, op1=ADD)


        ident = const.tile([P, P], F32, name="ident")
        make_identity(nc, ident[:])
        def units_of_step(step):
            row_units = [ROW_UNITS[n] for n in ROW_STEPS.get(step, [])]
            v_units = [(b, V_KIND, part) for b, part in V_LOADS.get(step, [])]
            return row_units, v_units

        load_order = ROW_UNITS[:ROW_HEAD]
        for step in range(TILES):
            row_units, v_units = units_of_step(step)
            load_order += row_units + v_units
        load_unit(load_order[0], slice(0, 1))
        for place in range(1, RAW_RING):
            load_unit(load_order[place])
            if place == ROW_HEAD - 1:
                load_unit(load_order[0], slice(1, 2))
            pair, odd = divmod(place - (ROW_HEAD - 1), 2)
            if 0 <= pair < TILES_PER_BATCH // 2 and odd == 0:
                load_bias(pair)

        def load_behind(unit):
            place = load_order.index(unit) + RAW_RING
            if place < len(load_order):
                load_unit(load_order[place])

        on_both = (on_scalar, on_vector)
        first_q = ROW_UNITS[0]
        group_q(first_q, 0, flip_q(first_q, 0, "flipped"), on_scalar)
        prepare_rows(ROW_UNITS[1], "scores", on_both)
        quantise_unit(first_q, 0, UNIT_WORDS // 2)
        prepare_rows(ROW_UNITS[2], "attn_t", on_both)
        quantise_unit(ROW_UNITS[1])
        prepare_rows(ROW_UNITS[3], "context", on_both)
        quantise_unit(ROW_UNITS[2])
        prepare_rows(ROW_UNITS[4], "scores", on_both)
        quantise_unit(ROW_UNITS[3])
        quantise_unit(ROW_UNITS[4])
        group_q(first_q, 1, flip_q(first_q, 1, "flipped"), on_scalar)
        score_matmuls(0)
        load_behind(first_q)

        def live(i):
            return 0 <= i < TILES

        for step in range(TILES):
            row_units, v_units = units_of_step(step)
            for unit in row_units:
                prepare_rows(unit, "flipped", (on_scalar, on_scalar))
            if step >= 5:
                halves_done = divmod(step - 5, 2)
                context_matmuls(*halves_done)
            if step >= 3:
                group_attn(step - 3, (on_scalar, on_scalar))
            if live(step):
                add_bias(step)
                if step == TILES - 1:
                    invert_sum(step - 1)
                    normalise(step - 1, nc.gpsimd.tensor_scalar)
                if step == 0:
                    quantise_unit(first_q, UNIT_WORDS // 2, UNIT_WORDS)
                find_maxima(step)
            if step == TILES - 1:
                find_shift(step)
            for unit in row_units:
                quantise_unit(unit)
            for b, part in V_LATE.get(step, []):
                quantise_unit((b, V_KIND, part))
            if step >= 3:
                quantise_attn(step - 3)
            if step < TILES - 1:
                find_shift(step)
            if live(step + 1):
                score_matmuls(step + 1)
            if step >= 2:
                transpose_attn(step - 2)
            for b, part, engine, first, last in V_PLAN.get(step, []):
                group_v((b, V_KIND, part), {"S": on_scalar, "V": on_vector, "G": on_gpsimd}[engine], first, last)
                if last == BANK:
                    load_behind((b, V_KIND, part))
            if step >= 5:
                copy_context(*halves_done, 0, on_scalar)
            if live(step):
                exponentials(step)
            for b, part in V_QUANT.get(step, []):
                quantise_unit((b, V_KIND, part))
            if live(step - 1) and step < TILES - 1:
                invert_sum(step - 1)
                normalise(step - 1, nc.gpsimd.tensor_scalar)
            if step >= 5:
                copy_context(*halves_done, 1, on_vector if step in CTX_V else on_scalar)

        last = TILES - 1
        end = last // 2
        context_matmuls(end - 2, 1)
        transpose_attn(last - 1, "scores")
        group_attn(last - 2, on_both)
        quantise_attn(last - 2)
        invert_sum(last)
        normalise(last, nc.vector.tensor_scalar)
        context_matmuls(end - 1, 0, "flipped")
        transpose_attn(last)
        group_attn(last - 1, on_both)
        quantise_attn(last - 1)
        for c in range(2):
            copy_context(end - 2, 1, c, on_both[c])
        group_attn(last, on_both)
        quantise_attn(last)
        context_matmuls(end - 1, 1)
        for c in range(2):
            copy_context(end - 1, 0, c, on_both[c])
        context_matmuls(end, 0, "scores")
        for c in range(2):
            copy_context(end - 1, 1, c, on_both[c])
        context_matmuls(end, 1, "flipped")
        for half in range(2):
            for c in range(2):
                copy_context(end, half, c, on_both[c])
